import numpy as np
import ml_dtypes


def mxq(x, axis, fmt="e4m3"):
    dtype, down = {"e4m3": (ml_dtypes.float8_e4m3fn, 7), "e5m2": (ml_dtypes.float8_e5m2, 14)}[fmt]
    v = np.moveaxis(np.asarray(x, np.float32).astype(ml_dtypes.bfloat16).astype(np.float64), axis, -1)
    blocks = v.reshape(v.shape[:-1] + (-1, 32))
    amax = np.abs(blocks).max(-1, keepdims=True)
    byte = np.maximum(np.where(amax > 0, np.frexp(amax)[1] - 1 + 127, 0) - down, 1)
    scale = np.exp2(byte - 127.0)
    codes = (blocks / scale).astype(np.float32).astype(dtype).astype(np.float64)
    return np.moveaxis((codes * scale).reshape(v.shape), -1, axis)


WIDE = False


def mx_kscale(k):
    if not WIDE:
        return np.ones(k)
    levels = np.array([20, -20, 10, -10, 0])
    a = np.random.permutation(np.resize(levels, k // 512 * 4)).reshape(k // 512, 4)
    idx = np.arange(k)
    return np.exp2(a[idx // 512, idx % 128 // 32])


BF16 = ml_dtypes.bfloat16


def bf(x):
    return np.asarray(x, np.float32).astype(BF16)


def f64(x):
    return np.asarray(x).astype(np.float64)


B, S, C, O, G = 4, 2048, 512, 512, 128
NG = C // G
T = B * S
SCALE_MIN = 1e-8


def setup_inputs():
    s = mx_kscale(T).reshape(B, S, 1)
    bound = 1.0 / np.sqrt(C)
    x = np.random.standard_normal((B, S, C)) * s
    weight = np.where(np.random.uniform(-bound, bound, (O, C)) >= 0, 1.0, -1.0)
    scales = (1.0 + 0.5 * np.random.standard_normal((O, NG))) / np.sqrt(C)
    g = np.random.standard_normal((B, S, O)) * np.exp2(np.random.randint(-12, 1, (B, S, 1))) / s
    return {"x": bf(x), "weight": bf(weight), "scales": bf(scales), "grad_out": bf(g)}


def reference(x, weight, scales, grad_out):
    xt = f64(x).reshape(T, C)
    gt = f64(grad_out).reshape(T, O)
    gwq = mxq(gt, 0, "e5m2").T @ mxq(xt, 0, "e4m3")
    sc = np.maximum(f64(scales), SCALE_MIN)
    return gwq * np.repeat(sc, G, axis=1)

@@ -1,0 +1,129 @@
+from contextlib import ExitStack
+
+import concourse.mybir as mybir
+
+BF16 = mybir.dt.bfloat16
+F32 = mybir.dt.float32
+U32 = mybir.dt.uint32
+U8 = mybir.dt.uint8
+E4M3_X4 = mybir.dt.float8_e4m3fn_x4
+E5M2_X4 = mybir.dt.float8_e5m2_x4
+COPY = mybir.ActivationFunctionType.Copy
+
+P = 128
+PACK = 4
+K_PASS = P * PACK
+TOKENS = 4 * 2048
+PASSES = TOKENS // K_PASS
+C_IN = 512
+C_OUT = 512
+GROUP = 128
+N_GROUPS = C_IN // GROUP
+M_TILES = C_OUT // P
+RUN = 4
+SCALE_MIN = 1e-8
+
+FLOPS = 2 * TOKENS * C_IN * C_OUT
+BYTES = 2 * TOKENS * (C_IN + C_OUT) + 2 * C_OUT * N_GROUPS + 4 * C_OUT * C_IN
+
+
+def regroup(copy, grouped, raw):
+    copy(
+        out=grouped[:].rearrange("p (c i) j -> p c j i", i=RUN),
+        in_=raw[:].rearrange("p j (c i) -> p c j i", i=RUN),
+    )
+
+
+def tile_literatiquantlinear_t_kernel(tc, x, weight, scales, grad_out, out):
+    nc = tc.nc
+    x_passes = x.flatten_outer_dims().rearrange("(c p j) w -> c p j w", p=P, j=PACK)
+    g_passes = grad_out.flatten_outer_dims().rearrange("(c p j) w -> c p j w", p=P, j=PACK)
+
+    with ExitStack() as ctx:
+        consts = ctx.enter_context(tc.tile_pool(name="consts", bufs=1))
+        landing = ctx.enter_context(tc.tile_pool(name="landing", bufs=PASSES))
+        staging = ctx.enter_context(tc.tile_pool(name="staging", bufs=3))
+        results = ctx.enter_context(tc.tile_pool(name="results", bufs=M_TILES))
+        psum = ctx.enter_context(tc.psum_pool(name="psum", bufs=1))
+        ctx.enter_context(tc.manual_schedule())
+
+        zero = consts.tile([P, 1], F32)
+        nc.vector.memset(zero[:], 0.0)
+        dummy = consts.tile([P, 1], F32)
+        nc.scalar.activation(out=dummy[:], in_=zero[:], func=COPY)
+
+        scales_bf16 = consts.tile([P, M_TILES, N_GROUPS], BF16)
+        nc.scalar.dma_start(out=scales_bf16[:], in_=scales.rearrange("(m p) g -> p m g", p=P))
+
+        g_raw = []
+        x_raw = []
+        for c in range(PASSES):
+            g_landing = landing.tile([P, PACK, C_OUT], BF16)
+            nc.sync.dma_start(out=g_landing[:], in_=g_passes[c])
+            g_raw.append(g_landing)
+            x_landing = landing.tile([P, PACK, C_IN], BF16)
+            nc.sync.dma_start(out=x_landing[:], in_=x_passes[c])
+            x_raw.append(x_landing)
+
+        acc = [psum.tile([P, C_IN], F32, name="acc%d" % m) for m in range(M_TILES)]
+
+        def finish_pass(c, g_grouped, x_codes, x_scales):
+            g_codes = staging.tile([P, C_OUT], U32, align_bytes=64)
+            g_scales = staging.tile([P, C_OUT], U8, align_bytes=64)
+            nc.vector.quantize_mx(
+                out=g_codes[:].bitcast(E5M2_X4),
+                scales=g_scales[:],
+                in_=g_grouped[:].rearrange("p w j -> p (w j)"),
+            )
+            for m in range(M_TILES):
+                m_cols = slice(m * P, (m + 1) * P)
+                nc.tensor.matmul_mx(
+                    out=acc[m][:],
+                    lhsT=g_codes[:, m_cols].bitcast(E5M2_X4),
+                    lhsT_scale=g_scales[:, m_cols],
+                    rhs=x_codes[:].bitcast(E4M3_X4),
+                    rhs_scale=x_scales[:],
+                    start=(c == 0),
+                    stop=(c == PASSES - 1),
+                )
+
+        unfinished = None
+        for c in range(PASSES):
+            g_grouped = staging.tile([P, C_OUT, PACK], BF16, align_bytes=64)
+            regroup(nc.scalar.copy, g_grouped, g_raw[c])
+            x_grouped = staging.tile([P, C_IN, PACK], BF16, align_bytes=64)
+            regroup(nc.vector.tensor_copy, x_grouped, x_raw[c])
+            if unfinished is not None:
+                finish_pass(*unfinished)
+            x_codes = staging.tile([P, C_IN], U32, align_bytes=64)
+            x_scales = staging.tile([P, C_IN], U8, align_bytes=64)
+            nc.vector.quantize_mx(
+                out=x_codes[:].bitcast(E4M3_X4),
+                scales=x_scales[:],
+                in_=x_grouped[:].rearrange("p w j -> p (w j)"),
+            )
+            unfinished = (c, g_grouped, x_codes, x_scales)
+        finish_pass(*unfinished)
+
+        clamped = consts.tile([P, M_TILES, N_GROUPS], F32)
+        nc.vector.tensor_scalar_max(out=clamped[:], in0=scales_bf16[:], scalar1=SCALE_MIN)
+
+        for m in range(M_TILES):
+            result = results.tile([P, C_IN], F32)
+            if m % 2 == 0:
+                nc.vector.tensor_tensor(
+                    out=result[:].rearrange("p (g w) -> p g w", g=N_GROUPS),
+                    in0=acc[m][:].rearrange("p (g w) -> p g w", g=N_GROUPS),
+                    in1=clamped[:, m, :].unsqueeze(2).to_broadcast([P, N_GROUPS, GROUP]),
+                    op=mybir.AluOpType.mult,
+                )
+            else:
+                for g in range(N_GROUPS):
+                    g_cols = slice(g * GROUP, (g + 1) * GROUP)
+                    nc.scalar.activation(
+                        out=result[:, g_cols],
+                        in_=acc[m][:, g_cols],
+                        func=COPY,
+                        scale=clamped[:, m, g : g + 1],
+                    )
+            nc.sync.dma_start(out=out[m * P : (m + 1) * P, :], in_=result[:])

@@ -29,8 +29,8 @@ BYTES = 2 * TOKENS * (C_IN + C_OUT) + 2 * C_OUT * N_GROUPS + 4 * C_OUT * C_IN
 
 def regroup(copy, grouped, raw):
     copy(
-        out=grouped[:].rearrange("p (c i) j -> p c j i", i=RUN),
-        in_=raw[:].rearrange("p j (c i) -> p c j i", i=RUN),
+        out=grouped.rearrange("p (c i) j -> p c j i", i=RUN),
+        in_=raw.rearrange("p j (c i) -> p c j i", i=RUN),
     )
 
 
@@ -55,46 +55,36 @@ def tile_literatiquantlinear_t_kernel(tc, x, weight, scales, grad_out, out):
         scales_bf16 = consts.tile([P, M_TILES, N_GROUPS], BF16)
         nc.scalar.dma_start(out=scales_bf16[:], in_=scales.rearrange("(m p) g -> p m g", p=P))
 
-        g_raw = []
         x_raw = []
+        g_raw = []
         for c in range(PASSES):
-            g_landing = landing.tile([P, PACK, C_OUT], BF16)
-            nc.sync.dma_start(out=g_landing[:], in_=g_passes[c])
-            g_raw.append(g_landing)
             x_landing = landing.tile([P, PACK, C_IN], BF16)
             nc.sync.dma_start(out=x_landing[:], in_=x_passes[c])
             x_raw.append(x_landing)
+            g_landing = landing.tile([P, PACK, C_OUT], BF16)
+            nc.sync.dma_start(out=g_landing[:], in_=g_passes[c])
+            g_raw.append(g_landing)
 
         acc = [psum.tile([P, C_IN], F32, name="acc%d" % m) for m in range(M_TILES)]
 
-        def finish_pass(c, g_grouped, x_codes, x_scales):
-            g_codes = staging.tile([P, C_OUT], U32, align_bytes=64)
-            g_scales = staging.tile([P, C_OUT], U8, align_bytes=64)
-            nc.vector.quantize_mx(
-                out=g_codes[:].bitcast(E5M2_X4),
-                scales=g_scales[:],
-                in_=g_grouped[:].rearrange("p w j -> p (w j)"),
-            )
-            for m in range(M_TILES):
-                m_cols = slice(m * P, (m + 1) * P)
-                nc.tensor.matmul_mx(
-                    out=acc[m][:],
-                    lhsT=g_codes[:, m_cols].bitcast(E5M2_X4),
-                    lhsT_scale=g_scales[:, m_cols],
-                    rhs=x_codes[:].bitcast(E4M3_X4),
-                    rhs_scale=x_scales[:],
-                    start=(c == 0),
-                    stop=(c == PASSES - 1),
-                )
+        def g_pieces(c):
+            if c == PASSES - 1:
+                return [[m] for m in range(M_TILES)]
+            return [list(range(M_TILES))]
 
-        unfinished = None
-        for c in range(PASSES):
-            g_grouped = staging.tile([P, C_OUT, PACK], BF16, align_bytes=64)
-            regroup(nc.scalar.copy, g_grouped, g_raw[c])
+        def columns(piece):
+            return slice(piece[0] * P, (piece[-1] + 1) * P)
+
+        def regroup_pass(c):
             x_grouped = staging.tile([P, C_IN, PACK], BF16, align_bytes=64)
-            regroup(nc.vector.tensor_copy, x_grouped, x_raw[c])
-            if unfinished is not None:
-                finish_pass(*unfinished)
+            regroup(nc.vector.tensor_copy, x_grouped[:], x_raw[c][:])
+            g_grouped = staging.tile([P, C_OUT, PACK], BF16, align_bytes=64)
+            for piece in g_pieces(c):
+                cols = columns(piece)
+                regroup(nc.scalar.copy, g_grouped[:, cols, :], g_raw[c][:, :, cols])
+            return x_grouped, g_grouped
+
+        def quantise_x(x_grouped):
             x_codes = staging.tile([P, C_IN], U32, align_bytes=64)
             x_scales = staging.tile([P, C_IN], U8, align_bytes=64)
             nc.vector.quantize_mx(
@@ -102,22 +92,44 @@ def tile_literatiquantlinear_t_kernel(tc, x, weight, scales, grad_out, out):
                 scales=x_scales[:],
                 in_=x_grouped[:].rearrange("p w j -> p (w j)"),
             )
-            unfinished = (c, g_grouped, x_codes, x_scales)
-        finish_pass(*unfinished)
+            return x_codes, x_scales
 
+        def finish_pass(c, g_grouped, x_codes, x_scales):
+            g_codes = staging.tile([P, C_OUT], U32, align_bytes=64)
+            g_scales = staging.tile([P, C_OUT], U8, align_bytes=64)
+            for piece in g_pieces(c):
+                cols = columns(piece)
+                nc.vector.quantize_mx(
+                    out=g_codes[:, cols].bitcast(E5M2_X4),
+                    scales=g_scales[:, cols],
+                    in_=g_grouped[:, cols, :].rearrange("p w j -> p (w j)"),
+                )
+                for m in piece:
+                    m_cols = columns([m])
+                    nc.tensor.matmul_mx(
+                        out=acc[m][:],
+                        lhsT=g_codes[:, m_cols].bitcast(E5M2_X4),
+                        lhsT_scale=g_scales[:, m_cols],
+                        rhs=x_codes[:].bitcast(E4M3_X4),
+                        rhs_scale=x_scales[:],
+                        start=(c == 0),
+                        stop=(c == PASSES - 1),
+                    )
+
+        x_grouped, g_grouped = regroup_pass(0)
+        x_codes, x_scales = quantise_x(x_grouped)
         clamped = consts.tile([P, M_TILES, N_GROUPS], F32)
         nc.vector.tensor_scalar_max(out=clamped[:], in0=scales_bf16[:], scalar1=SCALE_MIN)
+        for c in range(1, PASSES):
+            x_grouped, next_g_grouped = regroup_pass(c)
+            finish_pass(c - 1, g_grouped, x_codes, x_scales)
+            x_codes, x_scales = quantise_x(x_grouped)
+            g_grouped = next_g_grouped
+        finish_pass(PASSES - 1, g_grouped, x_codes, x_scales)
 
         for m in range(M_TILES):
             result = results.tile([P, C_IN], F32)
             if m % 2 == 0:
-                nc.vector.tensor_tensor(
-                    out=result[:].rearrange("p (g w) -> p g w", g=N_GROUPS),
-                    in0=acc[m][:].rearrange("p (g w) -> p g w", g=N_GROUPS),
-                    in1=clamped[:, m, :].unsqueeze(2).to_broadcast([P, N_GROUPS, GROUP]),
-                    op=mybir.AluOpType.mult,
-                )
-            else:
                 for g in range(N_GROUPS):
                     g_cols = slice(g * GROUP, (g + 1) * GROUP)
                     nc.scalar.activation(
@@ -126,4 +138,11 @@ def tile_literatiquantlinear_t_kernel(tc, x, weight, scales, grad_out, out):
                         func=COPY,
                         scale=clamped[:, m, g : g + 1],
                     )
+            else:
+                nc.vector.tensor_tensor(
+                    out=result[:].rearrange("p (g w) -> p g w", g=N_GROUPS),
+                    in0=acc[m][:].rearrange("p (g w) -> p g w", g=N_GROUPS),
+                    in1=clamped[:, m, :].unsqueeze(2).to_broadcast([P, N_GROUPS, GROUP]),
+                    op=mybir.AluOpType.mult,
+                )
             nc.sync.dma_start(out=out[m * P : (m + 1) * P, :], in_=result[:])

@@ -22,6 +22,7 @@ N_GROUPS = C_IN // GROUP
 M_TILES = C_OUT // P
 RUN = 4
 SCALE_MIN = 1e-8
+PIECED = 2
 
 FLOPS = 2 * TOKENS * C_IN * C_OUT
 BYTES = 2 * TOKENS * (C_IN + C_OUT) + 2 * C_OUT * N_GROUPS + 4 * C_OUT * C_IN
@@ -43,7 +44,7 @@ def tile_literatiquantlinear_t_kernel(tc, x, weight, scales, grad_out, out):
         consts = ctx.enter_context(tc.tile_pool(name="consts", bufs=1))
         landing = ctx.enter_context(tc.tile_pool(name="landing", bufs=PASSES))
         staging = ctx.enter_context(tc.tile_pool(name="staging", bufs=3))
-        results = ctx.enter_context(tc.tile_pool(name="results", bufs=M_TILES))
+        results = ctx.enter_context(tc.tile_pool(name="results", bufs=M_TILES + 1))
         psum = ctx.enter_context(tc.psum_pool(name="psum", bufs=1))
         ctx.enter_context(tc.manual_schedule())
 
@@ -51,9 +52,6 @@ def tile_literatiquantlinear_t_kernel(tc, x, weight, scales, grad_out, out):
         nc.vector.memset(zero[:], 0.0)
         dummy = consts.tile([P, 1], F32)
         nc.scalar.activation(out=dummy[:], in_=zero[:], func=COPY)
-
-        scales_bf16 = consts.tile([P, M_TILES, N_GROUPS], BF16)
-        nc.scalar.dma_start(out=scales_bf16[:], in_=scales.rearrange("(m p) g -> p m g", p=P))
 
         x_raw = []
         g_raw = []
@@ -65,24 +63,30 @@ def tile_literatiquantlinear_t_kernel(tc, x, weight, scales, grad_out, out):
             nc.sync.dma_start(out=g_landing[:], in_=g_passes[c])
             g_raw.append(g_landing)
 
+        scales_bf16 = consts.tile([P, M_TILES, N_GROUPS], BF16)
+        nc.sync.dma_start(out=scales_bf16[:], in_=scales.rearrange("(m p) g -> p m g", p=P))
+
         acc = [psum.tile([P, C_IN], F32, name="acc%d" % m) for m in range(M_TILES)]
 
         def g_pieces(c):
-            if c == PASSES - 1:
+            if c >= PASSES - PIECED:
                 return [[m] for m in range(M_TILES)]
             return [list(range(M_TILES))]
 
         def columns(piece):
             return slice(piece[0] * P, (piece[-1] + 1) * P)
 
-        def regroup_pass(c):
-            x_grouped = staging.tile([P, C_IN, PACK], BF16, align_bytes=64)
-            regroup(nc.vector.tensor_copy, x_grouped[:], x_raw[c][:])
+        def regroup_g(c):
             g_grouped = staging.tile([P, C_OUT, PACK], BF16, align_bytes=64)
             for piece in g_pieces(c):
                 cols = columns(piece)
                 regroup(nc.scalar.copy, g_grouped[:, cols, :], g_raw[c][:, :, cols])
-            return x_grouped, g_grouped
+            return g_grouped
+
+        def regroup_pass(c):
+            x_grouped = staging.tile([P, C_IN, PACK], BF16, align_bytes=64)
+            regroup(nc.vector.tensor_copy, x_grouped[:], x_raw[c][:])
+            return x_grouped, regroup_g(c)
 
         def quantise_x(x_grouped):
             x_codes = staging.tile([P, C_IN], U32, align_bytes=64)
@@ -94,55 +98,90 @@ def tile_literatiquantlinear_t_kernel(tc, x, weight, scales, grad_out, out):
             )
             return x_codes, x_scales
 
-        def finish_pass(c, g_grouped, x_codes, x_scales):
+        def g_code_tiles():
             g_codes = staging.tile([P, C_OUT], U32, align_bytes=64)
             g_scales = staging.tile([P, C_OUT], U8, align_bytes=64)
-            for piece in g_pieces(c):
-                cols = columns(piece)
-                nc.vector.quantize_mx(
-                    out=g_codes[:, cols].bitcast(E5M2_X4),
-                    scales=g_scales[:, cols],
-                    in_=g_grouped[:, cols, :].rearrange("p w j -> p (w j)"),
+            return g_codes, g_scales
+
+        def finish_piece(c, piece, g_grouped, g_quantised, x_quantised):
+            g_codes, g_scales = g_quantised
+            x_codes, x_scales = x_quantised
+            cols = columns(piece)
+            nc.vector.quantize_mx(
+                out=g_codes[:, cols].bitcast(E5M2_X4),
+                scales=g_scales[:, cols],
+                in_=g_grouped[:, cols, :].rearrange("p w j -> p (w j)"),
+            )
+            for m in piece:
+                m_cols = columns([m])
+                nc.tensor.matmul_mx(
+                    out=acc[m][:],
+                    lhsT=g_codes[:, m_cols].bitcast(E5M2_X4),
+                    lhsT_scale=g_scales[:, m_cols],
+                    rhs=x_codes[:].bitcast(E4M3_X4),
+                    rhs_scale=x_scales[:],
+                    start=(c == 0),
+                    stop=(c == PASSES - 1),
                 )
-                for m in piece:
-                    m_cols = columns([m])
-                    nc.tensor.matmul_mx(
-                        out=acc[m][:],
-                        lhsT=g_codes[:, m_cols].bitcast(E5M2_X4),
-                        lhsT_scale=g_scales[:, m_cols],
-                        rhs=x_codes[:].bitcast(E4M3_X4),
-                        rhs_scale=x_scales[:],
-                        start=(c == 0),
-                        stop=(c == PASSES - 1),
-                    )
+
+        def finish_pass(c, g_grouped, x_quantised):
+            g_quantised = g_code_tiles()
+            for piece in g_pieces(c):
+                finish_piece(c, piece, g_grouped, g_quantised, x_quantised)
 
         x_grouped, g_grouped = regroup_pass(0)
-        x_codes, x_scales = quantise_x(x_grouped)
-        clamped = consts.tile([P, M_TILES, N_GROUPS], F32)
-        nc.vector.tensor_scalar_max(out=clamped[:], in0=scales_bf16[:], scalar1=SCALE_MIN)
-        for c in range(1, PASSES):
+        x_quantised = quantise_x(x_grouped)
+        for c in range(1, PASSES - 1):
             x_grouped, next_g_grouped = regroup_pass(c)
-            finish_pass(c - 1, g_grouped, x_codes, x_scales)
-            x_codes, x_scales = quantise_x(x_grouped)
+            finish_pass(c - 1, g_grouped, x_quantised)
+            x_quantised = quantise_x(x_grouped)
             g_grouped = next_g_grouped
-        finish_pass(PASSES - 1, g_grouped, x_codes, x_scales)
 
-        for m in range(M_TILES):
-            result = results.tile([P, C_IN], F32)
-            if m % 2 == 0:
-                for g in range(N_GROUPS):
-                    g_cols = slice(g * GROUP, (g + 1) * GROUP)
+        last = PASSES - 1
+        half = C_IN // 2
+        last_g_grouped = regroup_g(last)
+        g_quantised = g_code_tiles()
+        x_grouped = staging.tile([P, C_IN, PACK], BF16, align_bytes=64)
+        finish_piece(last - 1, [0], g_grouped, g_quantised, x_quantised)
+        finish_piece(last - 1, [1], g_grouped, g_quantised, x_quantised)
+        regroup(nc.vector.tensor_copy, x_grouped[:, :half, :], x_raw[last][:, :, :half])
+        finish_piece(last - 1, [2], g_grouped, g_quantised, x_quantised)
+        regroup(nc.vector.tensor_copy, x_grouped[:, half:, :], x_raw[last][:, :, half:])
+        finish_piece(last - 1, [3], g_grouped, g_quantised, x_quantised)
+        x_quantised = quantise_x(x_grouped)
+        g_quantised = g_code_tiles()
+
+        clamped = consts.tile([P, M_TILES, N_GROUPS], F32)
+
+        def empty(engine, m, groups):
+            first = groups[0] * GROUP
+            width = len(groups) * GROUP
+            result = results.tile([P, width], F32)
+            if engine == "scalar":
+                for i, g in enumerate(groups):
                     nc.scalar.activation(
-                        out=result[:, g_cols],
-                        in_=acc[m][:, g_cols],
+                        out=result[:, i * GROUP : (i + 1) * GROUP],
+                        in_=acc[m][:, g * GROUP : (g + 1) * GROUP],
                         func=COPY,
                         scale=clamped[:, m, g : g + 1],
                     )
             else:
                 nc.vector.tensor_tensor(
-                    out=result[:].rearrange("p (g w) -> p g w", g=N_GROUPS),
-                    in0=acc[m][:].rearrange("p (g w) -> p g w", g=N_GROUPS),
-                    in1=clamped[:, m, :].unsqueeze(2).to_broadcast([P, N_GROUPS, GROUP]),
+                    out=result[:].rearrange("p (g w) -> p g w", w=GROUP),
+                    in0=acc[m][:, first : first + width].rearrange("p (g w) -> p g w", w=GROUP),
+                    in1=clamped[:, m, groups[0] : groups[-1] + 1].unsqueeze(2).to_broadcast([P, len(groups), GROUP]),
                     op=mybir.AluOpType.mult,
                 )
-            nc.sync.dma_start(out=out[m * P : (m + 1) * P, :], in_=result[:])
+            nc.sync.dma_start(out=out[m * P : (m + 1) * P, first : first + width], in_=result[:])
+
+        everything = list(range(N_GROUPS))
+        finish_piece(last, [0], last_g_grouped, g_quantised, x_quantised)
+        finish_piece(last, [1], last_g_grouped, g_quantised, x_quantised)
+        finish_piece(last, [2], last_g_grouped, g_quantised, x_quantised)
+        nc.vector.tensor_scalar_max(out=clamped[:], in0=scales_bf16[:], scalar1=SCALE_MIN)
+        empty("vector", 0, everything)
+        finish_piece(last, [3], last_g_grouped, g_quantised, x_quantised)
+        empty("scalar", 1, everything)
+        empty("vector", 2, everything)
+        empty("scalar", 3, everything[: N_GROUPS // 2])
+        empty("scalar", 3, everything[N_GROUPS // 2 :])

@@ -20,7 +20,7 @@ C_OUT = 512
 GROUP = 128
 N_GROUPS = C_IN // GROUP
 M_TILES = C_OUT // P
-RUN = 4
+RUN = 2
 SCALE_MIN = 1e-8
 PIECED = 2
 
@@ -183,5 +183,5 @@ def tile_literatiquantlinear_t_kernel(tc, x, weight, scales, grad_out, out):
         finish_piece(last, [3], last_g_grouped, g_quantised, x_quantised)
         empty("scalar", 1, everything)
         empty("vector", 2, everything)
-        empty("scalar", 3, everything[: N_GROUPS // 2])
-        empty("scalar", 3, everything[N_GROUPS // 2 :])
+        empty("vector", 3, everything[: N_GROUPS // 2])
+        empty("vector", 3, everything[N_GROUPS // 2 :])

from contextlib import ExitStack

import concourse.mybir as mybir

BF16 = mybir.dt.bfloat16
F32 = mybir.dt.float32
U32 = mybir.dt.uint32
U8 = mybir.dt.uint8
E4M3_X4 = mybir.dt.float8_e4m3fn_x4
E5M2_X4 = mybir.dt.float8_e5m2_x4
COPY = mybir.ActivationFunctionType.Copy

P = 128
PACK = 4
K_PASS = P * PACK
TOKENS = 4 * 2048
PASSES = TOKENS // K_PASS
C_IN = 512
C_OUT = 512
GROUP = 128
N_GROUPS = C_IN // GROUP
M_TILES = C_OUT // P
RUN = 2
SCALE_MIN = 1e-8
PIECED = 2

FLOPS = 2 * TOKENS * C_IN * C_OUT
BYTES = 2 * TOKENS * (C_IN + C_OUT) + 2 * C_OUT * N_GROUPS + 4 * C_OUT * C_IN


def regroup(copy, grouped, raw):
    copy(
        out=grouped.rearrange("p (c i) j -> p c j i", i=RUN),
        in_=raw.rearrange("p j (c i) -> p c j i", i=RUN),
    )


def tile_literatiquantlinear_t_kernel(tc, x, weight, scales, grad_out, out):
    nc = tc.nc
    x_passes = x.flatten_outer_dims().rearrange("(c p j) w -> c p j w", p=P, j=PACK)
    g_passes = grad_out.flatten_outer_dims().rearrange("(c p j) w -> c p j w", p=P, j=PACK)

    with ExitStack() as ctx:
        consts = ctx.enter_context(tc.tile_pool(name="consts", bufs=1))
        landing = ctx.enter_context(tc.tile_pool(name="landing", bufs=PASSES))
        staging = ctx.enter_context(tc.tile_pool(name="staging", bufs=3))
        results = ctx.enter_context(tc.tile_pool(name="results", bufs=M_TILES + 1))
        psum = ctx.enter_context(tc.psum_pool(name="psum", bufs=1))
        ctx.enter_context(tc.manual_schedule())

        zero = consts.tile([P, 1], F32)
        nc.vector.memset(zero[:], 0.0)
        dummy = consts.tile([P, 1], F32)
        nc.scalar.activation(out=dummy[:], in_=zero[:], func=COPY)

        x_raw = []
        g_raw = []
        for c in range(PASSES):
            x_landing = landing.tile([P, PACK, C_IN], BF16)
            nc.sync.dma_start(out=x_landing[:], in_=x_passes[c])
            x_raw.append(x_landing)
            g_landing = landing.tile([P, PACK, C_OUT], BF16)
            nc.sync.dma_start(out=g_landing[:], in_=g_passes[c])
            g_raw.append(g_landing)

        scales_bf16 = consts.tile([P, M_TILES, N_GROUPS], BF16)
        nc.sync.dma_start(out=scales_bf16[:], in_=scales.rearrange("(m p) g -> p m g", p=P))

        acc = [psum.tile([P, C_IN], F32, name="acc%d" % m) for m in range(M_TILES)]

        def g_pieces(c):
            if c >= PASSES - PIECED:
                return [[m] for m in range(M_TILES)]
            return [list(range(M_TILES))]

        def columns(piece):
            return slice(piece[0] * P, (piece[-1] + 1) * P)

        def regroup_g(c):
            g_grouped = staging.tile([P, C_OUT, PACK], BF16, align_bytes=64)
            for piece in g_pieces(c):
                cols = columns(piece)
                regroup(nc.scalar.copy, g_grouped[:, cols, :], g_raw[c][:, :, cols])
            return g_grouped

        def regroup_pass(c):
            x_grouped = staging.tile([P, C_IN, PACK], BF16, align_bytes=64)
            regroup(nc.vector.tensor_copy, x_grouped[:], x_raw[c][:])
            return x_grouped, regroup_g(c)

        def quantise_x(x_grouped):
            x_codes = staging.tile([P, C_IN], U32, align_bytes=64)
            x_scales = staging.tile([P, C_IN], U8, align_bytes=64)
            nc.vector.quantize_mx(
                out=x_codes[:].bitcast(E4M3_X4),
                scales=x_scales[:],
                in_=x_grouped[:].rearrange("p w j -> p (w j)"),
            )
            return x_codes, x_scales

        def g_code_tiles():
            g_codes = staging.tile([P, C_OUT], U32, align_bytes=64)
            g_scales = staging.tile([P, C_OUT], U8, align_bytes=64)
            return g_codes, g_scales

        def finish_piece(c, piece, g_grouped, g_quantised, x_quantised):
            g_codes, g_scales = g_quantised
            x_codes, x_scales = x_quantised
            cols = columns(piece)
            nc.vector.quantize_mx(
                out=g_codes[:, cols].bitcast(E5M2_X4),
                scales=g_scales[:, cols],
                in_=g_grouped[:, cols, :].rearrange("p w j -> p (w j)"),
            )
            for m in piece:
                m_cols = columns([m])
                nc.tensor.matmul_mx(
                    out=acc[m][:],
                    lhsT=g_codes[:, m_cols].bitcast(E5M2_X4),
                    lhsT_scale=g_scales[:, m_cols],
                    rhs=x_codes[:].bitcast(E4M3_X4),
                    rhs_scale=x_scales[:],
                    start=(c == 0),
                    stop=(c == PASSES - 1),
                )

        def finish_pass(c, g_grouped, x_quantised):
            g_quantised = g_code_tiles()
            for piece in g_pieces(c):
                finish_piece(c, piece, g_grouped, g_quantised, x_quantised)

        x_grouped, g_grouped = regroup_pass(0)
        x_quantised = quantise_x(x_grouped)
        for c in range(1, PASSES - 1):
            x_grouped, next_g_grouped = regroup_pass(c)
            finish_pass(c - 1, g_grouped, x_quantised)
            x_quantised = quantise_x(x_grouped)
            g_grouped = next_g_grouped

        last = PASSES - 1
        half = C_IN // 2
        last_g_grouped = regroup_g(last)
        g_quantised = g_code_tiles()
        x_grouped = staging.tile([P, C_IN, PACK], BF16, align_bytes=64)
        finish_piece(last - 1, [0], g_grouped, g_quantised, x_quantised)
        finish_piece(last - 1, [1], g_grouped, g_quantised, x_quantised)
        regroup(nc.vector.tensor_copy, x_grouped[:, :half, :], x_raw[last][:, :, :half])
        finish_piece(last - 1, [2], g_grouped, g_quantised, x_quantised)
        regroup(nc.vector.tensor_copy, x_grouped[:, half:, :], x_raw[last][:, :, half:])
        finish_piece(last - 1, [3], g_grouped, g_quantised, x_quantised)
        x_quantised = quantise_x(x_grouped)
        g_quantised = g_code_tiles()

        clamped = consts.tile([P, M_TILES, N_GROUPS], F32)

        def empty(engine, m, groups):
            first = groups[0] * GROUP
            width = len(groups) * GROUP
            result = results.tile([P, width], F32)
            if engine == "scalar":
                for i, g in enumerate(groups):
                    nc.scalar.activation(
                        out=result[:, i * GROUP : (i + 1) * GROUP],
                        in_=acc[m][:, g * GROUP : (g + 1) * GROUP],
                        func=COPY,
                        scale=clamped[:, m, g : g + 1],
                    )
            else:
                nc.vector.tensor_tensor(
                    out=result[:].rearrange("p (g w) -> p g w", w=GROUP),
                    in0=acc[m][:, first : first + width].rearrange("p (g w) -> p g w", w=GROUP),
                    in1=clamped[:, m, groups[0] : groups[-1] + 1].unsqueeze(2).to_broadcast([P, len(groups), GROUP]),
                    op=mybir.AluOpType.mult,
                )
            nc.sync.dma_start(out=out[m * P : (m + 1) * P, first : first + width], in_=result[:])

        everything = list(range(N_GROUPS))
        finish_piece(last, [0], last_g_grouped, g_quantised, x_quantised)
        finish_piece(last, [1], last_g_grouped, g_quantised, x_quantised)
        finish_piece(last, [2], last_g_grouped, g_quantised, x_quantised)
        nc.vector.tensor_scalar_max(out=clamped[:], in0=scales_bf16[:], scalar1=SCALE_MIN)
        empty("vector", 0, everything)
        finish_piece(last, [3], last_g_grouped, g_quantised, x_quantised)
        empty("scalar", 1, everything)
        empty("vector", 2, everything)
        empty("vector", 3, everything[: N_GROUPS // 2])
        empty("vector", 3, everything[N_GROUPS // 2 :])
